import numpy as np
import ml_dtypes


def mxq(x, axis, fmt="e4m3"):
    dtype, down = {"e4m3": (ml_dtypes.float8_e4m3fn, 7), "e5m2": (ml_dtypes.float8_e5m2, 14)}[fmt]
    v = np.moveaxis(np.asarray(x, np.float32).astype(ml_dtypes.bfloat16).astype(np.float64), axis, -1)
    blocks = v.reshape(v.shape[:-1] + (-1, 32))
    amax = np.abs(blocks).max(-1, keepdims=True)
    byte = np.maximum(np.where(amax > 0, np.frexp(amax)[1] - 1 + 127, 0) - down, 1)
    scale = np.exp2(byte - 127.0)
    codes = (blocks / scale).astype(np.float32).astype(dtype).astype(np.float64)
    return np.moveaxis((codes * scale).reshape(v.shape), -1, axis)


WIDE = False


def mx_kscale(k):
    if not WIDE:
        return np.ones(k)
    levels = np.array([10, -10, 5, -5, 0])
    a = np.random.permutation(np.resize(levels, k // 512 * 4)).reshape(k // 512, 4)
    idx = np.arange(k)
    return np.exp2(a[idx // 512, idx % 128 // 32])


BF16 = ml_dtypes.bfloat16


def bf(x):
    return np.asarray(x, np.float32).astype(BF16)


def f64(x):
    return np.asarray(x).astype(np.float64)


B, T, I, H = 128, 64, 1024, 128


def sigmoid(v):
    return 1.0 / (1.0 + np.exp(-v))


def setup_inputs():
    s = mx_kscale(I)
    d = {"inputs": bf(np.random.standard_normal((B, T, I)) * s),
         "h0": bf(np.random.standard_normal((1, B, H))),
         "c0": bf(np.random.standard_normal((1, B, H)))}
    for ni, nh in (("ii", "hi"), ("if_", "hf"), ("io", "ho"), ("ig", "hg")):
        d["w_" + ni] = bf(np.random.standard_normal((H, I)) / np.sqrt(I) / s[None, :])
        d["b_" + ni] = bf(np.random.standard_normal((H, 1)) * 0.3)
        d["w_" + nh] = bf(np.random.standard_normal((H, H)) * 0.7 / np.sqrt(H))
        d["b_" + nh] = bf(np.random.standard_normal((H, 1)) * 0.3)
    return d


def reference(inputs, h0, c0, w_ii, b_ii, w_hi, b_hi, w_if_, b_if_, w_hf, b_hf, w_io, b_io, w_ho, b_ho, w_ig, b_ig, w_hg, b_hg):
    xq = mxq(f64(inputs), 2, "e4m3")
    h0s = f64(h0)[0]
    c0s = f64(c0)[0]
    zi = (xq @ mxq(f64(w_ii), 1, "e4m3").T) + (h0s @ f64(w_hi).T)[:, None, :] + f64(b_ii)[:, 0] + f64(b_hi)[:, 0]
    zf = (xq @ mxq(f64(w_if_), 1, "e4m3").T) + (h0s @ f64(w_hf).T)[:, None, :] + f64(b_if_)[:, 0] + f64(b_hf)[:, 0]
    zg = (xq @ mxq(f64(w_ig), 1, "e4m3").T) + (h0s @ f64(w_hg).T)[:, None, :] + f64(b_ig)[:, 0] + f64(b_hg)[:, 0]
    zo = (xq @ mxq(f64(w_io), 1, "e4m3").T) + (h0s @ f64(w_ho).T)[:, None, :] + f64(b_io)[:, 0] + f64(b_ho)[:, 0]
    i = sigmoid(zi)
    f = sigmoid(zf)
    g = np.tanh(zg)
    o = sigmoid(zo)
    c_next = f * c0s[:, None, :] + i * g
    h_next = o * np.tanh(c_next)
    hidden_seq = np.transpose(h_next, (1, 0, 2))
    h_last = hidden_seq[-1][None]
    c_last = c_next[:, -1][None]
    return hidden_seq, h_last, c_last

@@ -1,0 +1,217 @@
+from contextlib import ExitStack
+
+import concourse.mybir as mybir
+from concourse.masks import make_identity
+
+FP8X4 = mybir.dt.float8_e4m3fn_x4
+BF16 = mybir.dt.bfloat16
+F32 = mybir.dt.float32
+I32 = mybir.dt.int32
+U32 = mybir.dt.uint32
+U8 = mybir.dt.uint8
+ACT = mybir.ActivationFunctionType
+ALU = mybir.AluOpType
+
+B, T, I, H = 128, 64, 1024, 128
+P = 128
+G4 = 4 * H
+TC = 4
+NCH = T // TC
+XBUFS = 8
+FLOPS = 2 * B * T * I * G4 + 2 * B * H * G4
+
+
+def tile_naivelstm_pa_t_kernel(
+    tc, inputs, h0, c0, w_ii, b_ii, w_hi, b_hi, w_if_, b_if_, w_hf, b_hf,
+    w_io, b_io, w_ho, b_ho, w_ig, b_ig, w_hg, b_hg, out_0, out_1, out_2,
+):
+    nc = tc.nc
+    w_in = [w_ii, w_if_, w_io, w_ig]
+    w_hid = [w_hi, w_hf, w_ho, w_hg]
+    b_in = [b_ii, b_if_, b_io, b_ig]
+    b_hid = [b_hi, b_hf, b_ho, b_hg]
+
+    with ExitStack() as ctx:
+        consts = ctx.enter_context(tc.tile_pool(name="consts", bufs=1))
+        xpool = ctx.enter_context(tc.tile_pool(name="xpool", bufs=XBUFS))
+        gpool = ctx.enter_context(tc.tile_pool(name="gpool", bufs=2))
+        qpool = ctx.enter_context(tc.tile_pool(name="qpool", bufs=3))
+        zpool = ctx.enter_context(tc.tile_pool(name="zpool", bufs=5))
+        epool = ctx.enter_context(tc.tile_pool(name="epool", bufs=3))
+        ps_t = ctx.enter_context(tc.psum_pool(name="ps_t", bufs=4))
+        ps_z = ctx.enter_context(tc.psum_pool(name="ps_z", bufs=4))
+        ctx.enter_context(tc.manual_schedule())
+
+        x_tiles = {}
+        xg_tiles = {}
+        code_tiles = {}
+        zs_tiles = {}
+        cn_tiles = {}
+        th_tiles = {}
+
+        def load_x(c):
+            x_sb = xpool.tile([P, TC * I], BF16, name="x_sb")
+            nc.sync.dma_start(
+                out=x_sb[:],
+                in_=inputs[:, c * TC:(c + 1) * TC, :].rearrange("b t k -> b (t k)"),
+            )
+            x_tiles[c] = x_sb
+
+        w_sb = consts.tile([P, 4 * I], BF16, name="w_sb")
+        for q in range(4):
+            nc.sync.dma_start(out=w_sb[:, q * I:(q + 1) * I], in_=w_in[q])
+        load_x(0)
+        small = consts.tile([P, 5 * H], BF16, name="small")
+        nc.sync.dma_start(out=small[:, 0:H], in_=h0[0])
+        for q in range(4):
+            nc.sync.dma_start(out=small[:, (q + 1) * H:(q + 2) * H], in_=w_hid[q])
+        load_x(1)
+        brow = consts.tile([P, G4], BF16, name="brow")
+        nc.vector.memset(brow[:].bitcast(I32), 0)
+        for q in range(4):
+            nc.sync.dma_start(out=brow[0:1, q * H:(q + 1) * H], in_=b_in[q].rearrange("h o -> o h"))
+            nc.sync.dma_start(out=brow[1:2, q * H:(q + 1) * H], in_=b_hid[q].rearrange("h o -> o h"))
+        c0_bf = consts.tile([P, H], BF16, name="c0_bf")
+        nc.sync.dma_start(out=c0_bf[:], in_=c0[0])
+        for c in range(2, XBUFS):
+            load_x(c)
+
+        ident_f = consts.tile([P, P], F32, name="ident_f")
+        make_identity(nc, ident_f[:])
+        ident_b = consts.tile([P, P], BF16, name="ident_b")
+        make_identity(nc, ident_b[:])
+        ones = consts.tile([P, P], BF16, name="ones")
+        nc.vector.memset(ones[:], 1.0)
+        warm = consts.tile([P, 1], F32, name="warm")
+        nc.vector.memset(warm[:], 0.0)
+        warm_out = consts.tile([P, 1], F32, name="warm_out")
+        nc.scalar.activation(out=warm_out[:], in_=warm[:], func=ACT.Sigmoid)
+
+        def transpose_rows(words):
+            bank = ps_t.tile([P, 4 * P], F32, name="bank", tag="bank")
+            for s in range(4):
+                nc.tensor.transpose(bank[:, s * P:(s + 1) * P], words[:, s * P:(s + 1) * P], ident_f[:])
+            return bank
+
+        def copy_out(engine_copy, dst_words, bank):
+            engine_copy(out=dst_words, in_=bank[:].rearrange("p (g u c) -> p g c u", g=2, u=2, c=P))
+
+        wg = consts.tile([P, 2 * G4 * 4], BF16, name="wg", align_bytes=64)
+        wg_words = wg[:].bitcast(F32).rearrange("p (g c u) -> p g c u", g=2, c=G4, u=2)
+        w_words = w_sb[:].bitcast(F32)
+        for q in range(4):
+            bank = transpose_rows(w_words[:, q * 512:(q + 1) * 512])
+            copy_out(nc.vector.tensor_copy, wg_words[:, :, q * H:(q + 1) * H, :], bank)
+        w_codes = consts.tile([P, 2 * G4], U32, name="w_codes", align_bytes=64)
+        w_scales = consts.tile([P, 2 * G4], U8, name="w_scales", align_bytes=64)
+        nc.vector.quantize_mx(out=w_codes[:].bitcast(FP8X4), scales=w_scales[:], in_=wg[:])
+
+        r_sb = consts.tile([P, G4], F32, name="r_sb")
+        c0_f = consts.tile([P, H], F32, name="c0_f")
+
+        def make_r():
+            small_ps = ps_z.tile([P, 5 * H], BF16, name="small_ps", tag="z_ps")
+            for s in range(5):
+                nc.tensor.transpose(small_ps[:, s * H:(s + 1) * H], small[:, s * H:(s + 1) * H], ident_b[:])
+            small_t = consts.tile([P, 5 * H], BF16, name="small_t")
+            nc.vector.tensor_copy(out=small_t[:], in_=small_ps[:])
+            r_ps = ps_z.tile([P, G4], F32, name="r_ps", tag="z_ps")
+            nc.tensor.matmul(r_ps[:], lhsT=small_t[:, 0:H], rhs=small_t[:, H:5 * H], start=True, stop=False)
+            nc.tensor.matmul(r_ps[:], lhsT=ones[:], rhs=brow[:], start=False, stop=True)
+            nc.vector.tensor_copy(out=r_sb[:], in_=r_ps[:])
+            nc.vector.tensor_copy(out=c0_f[:], in_=c0_bf[:])
+
+        def stage_tp(c):
+            x_words = x_tiles[c][:].bitcast(F32)
+            xg = gpool.tile([P, TC * 2 * P * 4], BF16, name="xg", align_bytes=64)
+            xg_words = xg[:].bitcast(F32).rearrange("p (j g c u) -> p j g c u", j=TC, g=2, c=P, u=2)
+            for j in range(TC):
+                bank = transpose_rows(x_words[:, j * 512:(j + 1) * 512])
+                copy_out(nc.vector.tensor_copy if j == 0 else nc.scalar.copy, xg_words[:, j], bank)
+            xg_tiles[c] = xg
+            if c + XBUFS < NCH:
+                load_x(c + XBUFS)
+
+        def stage_q(c):
+            x_codes = qpool.tile([P, TC * 2 * P], U32, name="x_codes", align_bytes=64)
+            x_scales = qpool.tile([P, TC * 2 * P], U8, name="x_scales", align_bytes=64)
+            nc.vector.quantize_mx(out=x_codes[:].bitcast(FP8X4), scales=x_scales[:], in_=xg_tiles[c][:])
+            code_tiles[c] = (x_codes, x_scales)
+
+        def stage_mx(c):
+            x_codes, x_scales = code_tiles[c]
+            banks = []
+            for j in range(TC):
+                z_ps = ps_z.tile([P, G4], F32, name="z_ps", tag="z_ps")
+                for g in range(2):
+                    cols = slice((j * 2 + g) * P, (j * 2 + g + 1) * P)
+                    nc.tensor.matmul_mx(
+                        out=z_ps[:],
+                        lhsT=x_codes[:, cols].bitcast(FP8X4),
+                        lhsT_scale=x_scales[:, cols],
+                        rhs=w_codes[:, g * G4:(g + 1) * G4].bitcast(FP8X4),
+                        rhs_scale=w_scales[:, g * G4:(g + 1) * G4],
+                        start=(g == 0),
+                        stop=(g == 1),
+                    )
+                banks.append(z_ps)
+            zs = zpool.tile([P, TC, G4], F32, name="zs")
+            zs_tiles[c] = zs
+            return banks
+
+        def add_r(c, banks, j):
+            nc.vector.tensor_tensor(out=zs_tiles[c][:, j, :], in0=banks[j][:], in1=r_sb[:], op=ALU.add)
+
+        def stage_act(c):
+            zs = zs_tiles[c]
+            nc.scalar.activation(out=zs[:, :, 0:3 * H], in_=zs[:, :, 0:3 * H], func=ACT.Sigmoid)
+            nc.scalar.activation(out=zs[:, :, 3 * H:G4], in_=zs[:, :, 3 * H:G4], func=ACT.Tanh)
+
+        def stage_gate(c):
+            zs = zs_tiles[c]
+            ig = epool.tile([P, TC, H], F32, name="ig")
+            nc.gpsimd.tensor_tensor(out=ig[:], in0=zs[:, :, 0:H], in1=zs[:, :, 3 * H:G4], op=ALU.mult)
+            fc = epool.tile([P, TC, H], F32, name="fc")
+            nc.gpsimd.tensor_tensor(out=fc[:], in0=zs[:, :, H:2 * H],
+                                    in1=c0_f[:].unsqueeze(1).to_broadcast([P, TC, H]), op=ALU.mult)
+            cn = epool.tile([P, TC, H], F32, name="cn")
+            nc.gpsimd.tensor_tensor(out=cn[:], in0=fc[:], in1=ig[:], op=ALU.add)
+            cn_tiles[c] = cn
+
+        def stage_tanh_c(c):
+            th = epool.tile([P, TC, H], F32, name="th")
+            nc.scalar.activation(out=th[:], in_=cn_tiles[c][:], func=ACT.Tanh)
+            th_tiles[c] = th
+
+        def stage_out(c):
+            hn = epool.tile([P, TC, H], F32, name="hn")
+            nc.vector.tensor_tensor(out=hn[:], in0=zs_tiles[c][:, :, 2 * H:3 * H], in1=th_tiles[c][:], op=ALU.mult)
+            nc.sync.dma_start(out=out_0[c * TC:(c + 1) * TC].rearrange("t b h -> b t h"), in_=hn[:])
+            if c == NCH - 1:
+                nc.sync.dma_start(out=out_1[0], in_=hn[:, TC - 1, :])
+                nc.sync.dma_start(out=out_2[0], in_=cn_tiles[c][:, TC - 1, :])
+
+        def live(c):
+            return 0 <= c < NCH
+
+        for i in range(-1, NCH + 3):
+            if live(i + 1):
+                stage_tp(i + 1)
+            if i == -1:
+                make_r()
+            if live(i - 3):
+                stage_out(i - 3)
+            banks = stage_mx(i) if live(i) else None
+            if live(i):
+                add_r(i, banks, 0)
+                add_r(i, banks, 1)
+            if live(i + 1):
+                stage_q(i + 1)
+            if live(i):
+                add_r(i, banks, 2)
+                add_r(i, banks, 3)
+            if live(i - 1):
+                stage_act(i - 1)
+                stage_gate(i - 1)
+            if live(i - 2):
+                stage_tanh_c(i - 2)

@@ -15,9 +15,11 @@ ALU = mybir.AluOpType
 B, T, I, H = 128, 64, 1024, 128
 P = 128
 G4 = 4 * H
-TC = 4
-NCH = T // TC
-XBUFS = 8
+ROWS = 512
+NT = ROWS // P
+NB = ROWS // T
+NCH = B * T // ROWS
+XBUFS = 6
 FLOPS = 2 * B * T * I * G4 + 2 * B * H * G4
 
 
@@ -26,34 +28,44 @@ def tile_naivelstm_pa_t_kernel(
     w_io, b_io, w_ho, b_ho, w_ig, b_ig, w_hg, b_hg, out_0, out_1, out_2,
 ):
     nc = tc.nc
-    w_in = [w_ii, w_if_, w_io, w_ig]
-    w_hid = [w_hi, w_hf, w_ho, w_hg]
-    b_in = [b_ii, b_if_, b_io, b_ig]
-    b_hid = [b_hi, b_hf, b_ho, b_hg]
+    w_in = [w_ii, w_ig, w_if_, w_io]
+    w_hid = [w_hi, w_hg, w_hf, w_ho]
+    b_in = [b_ii, b_ig, b_if_, b_io]
+    b_hid = [b_hi, b_hg, b_hf, b_ho]
+    funcs = [ACT.Sigmoid, ACT.Tanh, ACT.Sigmoid, ACT.Sigmoid]
+
+    x_rows = inputs.rearrange("b t k -> (b t) k")
+    out_seq = out_0.rearrange("t (m e) h -> e t m h", e=2)
+    out_hl = out_1[0].rearrange("(m e) h -> e m h", e=2)
 
     with ExitStack() as ctx:
         consts = ctx.enter_context(tc.tile_pool(name="consts", bufs=1))
         xpool = ctx.enter_context(tc.tile_pool(name="xpool", bufs=XBUFS))
         gpool = ctx.enter_context(tc.tile_pool(name="gpool", bufs=2))
         qpool = ctx.enter_context(tc.tile_pool(name="qpool", bufs=3))
-        zpool = ctx.enter_context(tc.tile_pool(name="zpool", bufs=5))
+        spool = ctx.enter_context(tc.tile_pool(name="spool", bufs=4))
         epool = ctx.enter_context(tc.tile_pool(name="epool", bufs=3))
-        ps_t = ctx.enter_context(tc.psum_pool(name="ps_t", bufs=4))
-        ps_z = ctx.enter_context(tc.psum_pool(name="ps_z", bufs=4))
+        ps_t = ctx.enter_context(tc.psum_pool(name="ps_t", bufs=3))
+        ps_z = ctx.enter_context(tc.psum_pool(name="ps_z", bufs=1))
+        ps_o = ctx.enter_context(tc.psum_pool(name="ps_o", bufs=1))
         ctx.enter_context(tc.manual_schedule())
 
         x_tiles = {}
         xg_tiles = {}
         code_tiles = {}
-        zs_tiles = {}
+        z_tiles = {}
+        gate_tiles = {}
+        ig_tiles = {}
         cn_tiles = {}
         th_tiles = {}
+        ht_tiles = {}
+        ot_tiles = {}
 
         def load_x(c):
-            x_sb = xpool.tile([P, TC * I], BF16, name="x_sb")
+            x_sb = xpool.tile([P, NT * I], BF16, name="x_sb")
             nc.sync.dma_start(
-                out=x_sb[:],
-                in_=inputs[:, c * TC:(c + 1) * TC, :].rearrange("b t k -> b (t k)"),
+                out=x_sb[:].rearrange("p (n k) -> p n k", n=NT),
+                in_=x_rows[c * ROWS:(c + 1) * ROWS, :].rearrange("(n p) k -> p n k", p=P),
             )
             x_tiles[c] = x_sb
 
@@ -61,18 +73,17 @@ def tile_naivelstm_pa_t_kernel(
         for q in range(4):
             nc.sync.dma_start(out=w_sb[:, q * I:(q + 1) * I], in_=w_in[q])
         load_x(0)
-        small = consts.tile([P, 5 * H], BF16, name="small")
+        small = consts.tile([P, 6 * H], BF16, name="small")
         nc.sync.dma_start(out=small[:, 0:H], in_=h0[0])
         for q in range(4):
             nc.sync.dma_start(out=small[:, (q + 1) * H:(q + 2) * H], in_=w_hid[q])
+        nc.sync.dma_start(out=small[:, 5 * H:6 * H], in_=c0[0])
         load_x(1)
         brow = consts.tile([P, G4], BF16, name="brow")
         nc.vector.memset(brow[:].bitcast(I32), 0)
         for q in range(4):
             nc.sync.dma_start(out=brow[0:1, q * H:(q + 1) * H], in_=b_in[q].rearrange("h o -> o h"))
             nc.sync.dma_start(out=brow[1:2, q * H:(q + 1) * H], in_=b_hid[q].rearrange("h o -> o h"))
-        c0_bf = consts.tile([P, H], BF16, name="c0_bf")
-        nc.sync.dma_start(out=c0_bf[:], in_=c0[0])
         for c in range(2, XBUFS):
             load_x(c)
 
@@ -106,112 +117,139 @@ def tile_naivelstm_pa_t_kernel(
         w_scales = consts.tile([P, 2 * G4], U8, name="w_scales", align_bytes=64)
         nc.vector.quantize_mx(out=w_codes[:].bitcast(FP8X4), scales=w_scales[:], in_=wg[:])
 
-        r_sb = consts.tile([P, G4], F32, name="r_sb")
-        c0_f = consts.tile([P, H], F32, name="c0_f")
+        rt_sb = consts.tile([P, G4], F32, name="rt_sb")
+        c0t = consts.tile([P, B], F32, name="c0t")
+        clt = consts.tile([P, B], F32, name="clt")
 
         def make_r():
-            small_ps = ps_z.tile([P, 5 * H], BF16, name="small_ps", tag="z_ps")
-            for s in range(5):
+            small_ps = ps_t.tile([P, 6 * H], BF16, name="small_ps", tag="bank")
+            for s in range(6):
                 nc.tensor.transpose(small_ps[:, s * H:(s + 1) * H], small[:, s * H:(s + 1) * H], ident_b[:])
-            small_t = consts.tile([P, 5 * H], BF16, name="small_t")
+            small_t = consts.tile([P, 6 * H], BF16, name="small_t")
             nc.vector.tensor_copy(out=small_t[:], in_=small_ps[:])
-            r_ps = ps_z.tile([P, G4], F32, name="r_ps", tag="z_ps")
-            nc.tensor.matmul(r_ps[:], lhsT=small_t[:, 0:H], rhs=small_t[:, H:5 * H], start=True, stop=False)
-            nc.tensor.matmul(r_ps[:], lhsT=ones[:], rhs=brow[:], start=False, stop=True)
-            nc.vector.tensor_copy(out=r_sb[:], in_=r_ps[:])
-            nc.vector.tensor_copy(out=c0_f[:], in_=c0_bf[:])
+            rt_ps = ps_o.tile([P, G4], F32, name="rt_ps", tag="ot")
+            for q in range(4):
+                cols = slice(q * H, (q + 1) * H)
+                nc.tensor.matmul(rt_ps[:, cols], lhsT=small_t[:, (q + 1) * H:(q + 2) * H], rhs=small_t[:, 0:H],
+                                 start=True, stop=False)
+                nc.tensor.matmul(rt_ps[:, cols], lhsT=brow[:, cols], rhs=ones[:], start=False, stop=True)
+            nc.vector.tensor_copy(out=rt_sb[:], in_=rt_ps[:])
+            nc.vector.tensor_copy(out=c0t[:], in_=small_t[:, 5 * H:6 * H])
 
         def stage_tp(c):
             x_words = x_tiles[c][:].bitcast(F32)
-            xg = gpool.tile([P, TC * 2 * P * 4], BF16, name="xg", align_bytes=64)
-            xg_words = xg[:].bitcast(F32).rearrange("p (j g c u) -> p j g c u", j=TC, g=2, c=P, u=2)
-            for j in range(TC):
-                bank = transpose_rows(x_words[:, j * 512:(j + 1) * 512])
-                copy_out(nc.vector.tensor_copy if j == 0 else nc.scalar.copy, xg_words[:, j], bank)
+            xg = gpool.tile([P, 2 * ROWS * 4], BF16, name="xg", align_bytes=64)
+            xg_words = xg[:].bitcast(F32).rearrange("p (g c u) -> p g c u", g=2, c=ROWS, u=2)
+            for n in range(NT):
+                bank = transpose_rows(x_words[:, n * 512:(n + 1) * 512])
+                copy_out(nc.scalar.copy if n < 2 else nc.vector.tensor_copy,
+                         xg_words[:, :, n * P:(n + 1) * P, :], bank)
             xg_tiles[c] = xg
             if c + XBUFS < NCH:
                 load_x(c + XBUFS)
 
         def stage_q(c):
-            x_codes = qpool.tile([P, TC * 2 * P], U32, name="x_codes", align_bytes=64)
-            x_scales = qpool.tile([P, TC * 2 * P], U8, name="x_scales", align_bytes=64)
+            x_codes = qpool.tile([P, 2 * ROWS], U32, name="x_codes", align_bytes=64)
+            x_scales = qpool.tile([P, 2 * ROWS], U8, name="x_scales", align_bytes=64)
             nc.vector.quantize_mx(out=x_codes[:].bitcast(FP8X4), scales=x_scales[:], in_=xg_tiles[c][:])
             code_tiles[c] = (x_codes, x_scales)
 
         def stage_mx(c):
             x_codes, x_scales = code_tiles[c]
             banks = []
-            for j in range(TC):
-                z_ps = ps_z.tile([P, G4], F32, name="z_ps", tag="z_ps")
+            for q in range(4):
+                z_ps = ps_z.tile([P, ROWS], F32, name="z_ps%d" % q, tag="z_ps%d" % q)
                 for g in range(2):
-                    cols = slice((j * 2 + g) * P, (j * 2 + g + 1) * P)
+                    w_cols = slice(g * G4 + q * H, g * G4 + (q + 1) * H)
+                    x_cols = slice(g * ROWS, (g + 1) * ROWS)
                     nc.tensor.matmul_mx(
                         out=z_ps[:],
-                        lhsT=x_codes[:, cols].bitcast(FP8X4),
-                        lhsT_scale=x_scales[:, cols],
-                        rhs=w_codes[:, g * G4:(g + 1) * G4].bitcast(FP8X4),
-                        rhs_scale=w_scales[:, g * G4:(g + 1) * G4],
+                        lhsT=w_codes[:, w_cols].bitcast(FP8X4),
+                        lhsT_scale=w_scales[:, w_cols],
+                        rhs=x_codes[:, x_cols].bitcast(FP8X4),
+                        rhs_scale=x_scales[:, x_cols],
                         start=(g == 0),
                         stop=(g == 1),
                     )
                 banks.append(z_ps)
-            zs = zpool.tile([P, TC, G4], F32, name="zs")
-            zs_tiles[c] = zs
-            return banks
-
-        def add_r(c, banks, j):
-            nc.vector.tensor_tensor(out=zs_tiles[c][:, j, :], in0=banks[j][:], in1=r_sb[:], op=ALU.add)
+            z_tiles[c] = banks
 
         def stage_act(c):
-            zs = zs_tiles[c]
-            nc.scalar.activation(out=zs[:, :, 0:3 * H], in_=zs[:, :, 0:3 * H], func=ACT.Sigmoid)
-            nc.scalar.activation(out=zs[:, :, 3 * H:G4], in_=zs[:, :, 3 * H:G4], func=ACT.Tanh)
+            gates = []
+            for q in range(4):
+                gate = spool.tile([P, ROWS], F32, name="gate%d" % q, tag="gate%d" % q)
+                for bl in range(NB):
+                    cols = slice(bl * T, (bl + 1) * T)
+                    b = c * NB + bl
+                    nc.scalar.activation(out=gate[:, cols], in_=z_tiles[c][q][:, cols], func=funcs[q],
+                                         bias=rt_sb[:, q * B + b:q * B + b + 1])
+                gates.append(gate)
+            gate_tiles[c] = gates
 
-        def stage_gate(c):
-            zs = zs_tiles[c]
-            ig = epool.tile([P, TC, H], F32, name="ig")
-            nc.gpsimd.tensor_tensor(out=ig[:], in0=zs[:, :, 0:H], in1=zs[:, :, 3 * H:G4], op=ALU.mult)
-            fc = epool.tile([P, TC, H], F32, name="fc")
-            nc.gpsimd.tensor_tensor(out=fc[:], in0=zs[:, :, H:2 * H],
-                                    in1=c0_f[:].unsqueeze(1).to_broadcast([P, TC, H]), op=ALU.mult)
-            cn = epool.tile([P, TC, H], F32, name="cn")
-            nc.gpsimd.tensor_tensor(out=cn[:], in0=fc[:], in1=ig[:], op=ALU.add)
+        def stage_cell(c):
+            g_i, g_g, g_f, g_o = gate_tiles[c]
+            ig = epool.tile([P, ROWS], F32, name="ig")
+            nc.vector.tensor_tensor(out=ig[:], in0=g_i[:], in1=g_g[:], op=ALU.mult)
+            cn = epool.tile([P, ROWS], F32, name="cn")
+            for bl in range(NB):
+                cols = slice(bl * T, (bl + 1) * T)
+                b = c * NB + bl
+                nc.vector.scalar_tensor_tensor(out=cn[:, cols], in0=g_f[:, cols], scalar=c0t[:, b:b + 1],
+                                               in1=ig[:, cols], op0=ALU.mult, op1=ALU.add)
+            nc.vector.tensor_copy(out=clt[:, c * NB:(c + 1) * NB],
+                                  in_=cn[:].rearrange("p (b t) -> p b t", t=T)[:, :, T - 1])
             cn_tiles[c] = cn
 
         def stage_tanh_c(c):
-            th = epool.tile([P, TC, H], F32, name="th")
+            th = epool.tile([P, ROWS], F32, name="th")
             nc.scalar.activation(out=th[:], in_=cn_tiles[c][:], func=ACT.Tanh)
             th_tiles[c] = th
 
-        def stage_out(c):
-            hn = epool.tile([P, TC, H], F32, name="hn")
-            nc.vector.tensor_tensor(out=hn[:], in0=zs_tiles[c][:, :, 2 * H:3 * H], in1=th_tiles[c][:], op=ALU.mult)
-            nc.sync.dma_start(out=out_0[c * TC:(c + 1) * TC].rearrange("t b h -> b t h"), in_=hn[:])
-            if c == NCH - 1:
-                nc.sync.dma_start(out=out_1[0], in_=hn[:, TC - 1, :])
-                nc.sync.dma_start(out=out_2[0], in_=cn_tiles[c][:, TC - 1, :])
+        def stage_h(c):
+            ht = epool.tile([P, ROWS], F32, name="ht")
+            nc.vector.tensor_tensor(out=ht[:], in0=gate_tiles[c][3][:], in1=th_tiles[c][:], op=ALU.mult)
+            ht_tiles[c] = ht
+
+        def stage_ot(c):
+            ot = ps_o.tile([P, ROWS], F32, name="ot", tag="ot")
+            for n in range(NT):
+                nc.tensor.transpose(ot[:, n * P:(n + 1) * P], ht_tiles[c][:, n * P:(n + 1) * P], ident_f[:])
+            ot_tiles[c] = ot
+
+        def stage_store(c):
+            o_sb = epool.tile([P, NT, H], F32, name="o_sb")
+            nc.vector.tensor_copy(out=o_sb[:].rearrange("p n h -> p (n h)"), in_=ot_tiles[c][:])
+            for e in range(2):
+                nc.sync.dma_start(out=out_seq[e, :, c * NT:(c + 1) * NT, :], in_=o_sb[e * T:(e + 1) * T, :, :])
+            nc.sync.dma_start(out=out_hl[:, c * NT:(c + 1) * NT, :], in_=o_sb[T - 1:P:T, :, :])
 
         def live(c):
             return 0 <= c < NCH
 
-        for i in range(-1, NCH + 3):
+        for i in range(-1, NCH + 4):
+            if live(i - 1):
+                stage_cell(i - 1)
             if live(i + 1):
                 stage_tp(i + 1)
             if i == -1:
                 make_r()
             if live(i - 3):
-                stage_out(i - 3)
-            banks = stage_mx(i) if live(i) else None
+                stage_ot(i - 3)
             if live(i):
-                add_r(i, banks, 0)
-                add_r(i, banks, 1)
+                stage_mx(i)
+            if live(i - 2):
+                stage_h(i - 2)
             if live(i + 1):
                 stage_q(i + 1)
+            if live(i - 3):
+                stage_store(i - 3)
             if live(i):
-                add_r(i, banks, 2)
-                add_r(i, banks, 3)
+                stage_act(i)
             if live(i - 1):
-                stage_act(i - 1)
-                stage_gate(i - 1)
-            if live(i - 2):
-                stage_tanh_c(i - 2)
+                stage_tanh_c(i - 1)
+            if i == NCH:
+                cl_ps = ps_t.tile([P, H], F32, name="cl_ps", tag="bank")
+                nc.tensor.transpose(cl_ps[:], clt[:], ident_f[:])
+                cl_sb = consts.tile([P, H], F32, name="cl_sb")
+                nc.scalar.copy(out=cl_sb[:], in_=cl_ps[:])
+                nc.sync.dma_start(out=out_2[0], in_=cl_sb[:])

@@ -15,11 +15,9 @@ ALU = mybir.AluOpType
 B, T, I, H = 128, 64, 1024, 128
 P = 128
 G4 = 4 * H
-ROWS = 512
-NT = ROWS // P
-NB = ROWS // T
-NCH = B * T // ROWS
-XBUFS = 6
+TC = 4
+NCH = T // TC
+XBUFS = 8
 FLOPS = 2 * B * T * I * G4 + 2 * B * H * G4
 
 
@@ -28,64 +26,63 @@ def tile_naivelstm_pa_t_kernel(
     w_io, b_io, w_ho, b_ho, w_ig, b_ig, w_hg, b_hg, out_0, out_1, out_2,
 ):
     nc = tc.nc
-    w_in = [w_ii, w_ig, w_if_, w_io]
-    w_hid = [w_hi, w_hg, w_hf, w_ho]
-    b_in = [b_ii, b_ig, b_if_, b_io]
-    b_hid = [b_hi, b_hg, b_hf, b_ho]
-    funcs = [ACT.Sigmoid, ACT.Tanh, ACT.Sigmoid, ACT.Sigmoid]
-
-    x_rows = inputs.rearrange("b t k -> (b t) k")
-    out_seq = out_0.rearrange("t (m e) h -> e t m h", e=2)
-    out_hl = out_1[0].rearrange("(m e) h -> e m h", e=2)
+    w_in = [w_ii, w_if_, w_io, w_ig]
+    w_hid = [w_hi, w_hf, w_ho, w_hg]
+    b_in = [b_ii, b_if_, b_io, b_ig]
+    b_hid = [b_hi, b_hf, b_ho, b_hg]
 
     with ExitStack() as ctx:
         consts = ctx.enter_context(tc.tile_pool(name="consts", bufs=1))
         xpool = ctx.enter_context(tc.tile_pool(name="xpool", bufs=XBUFS))
-        gpool = ctx.enter_context(tc.tile_pool(name="gpool", bufs=2))
+        gpool = ctx.enter_context(tc.tile_pool(name="gpool", bufs=3))
         qpool = ctx.enter_context(tc.tile_pool(name="qpool", bufs=3))
-        spool = ctx.enter_context(tc.tile_pool(name="spool", bufs=4))
+        zpool = ctx.enter_context(tc.tile_pool(name="zpool", bufs=4))
+        ppool = ctx.enter_context(tc.tile_pool(name="ppool", bufs=1))
         epool = ctx.enter_context(tc.tile_pool(name="epool", bufs=3))
-        ps_t = ctx.enter_context(tc.psum_pool(name="ps_t", bufs=3))
-        ps_z = ctx.enter_context(tc.psum_pool(name="ps_z", bufs=1))
-        ps_o = ctx.enter_context(tc.psum_pool(name="ps_o", bufs=1))
+        ps_t = ctx.enter_context(tc.psum_pool(name="ps_t", bufs=4))
+        ps_z = ctx.enter_context(tc.psum_pool(name="ps_z", bufs=4))
         ctx.enter_context(tc.manual_schedule())
 
         x_tiles = {}
+        bank_tiles = {}
         xg_tiles = {}
         code_tiles = {}
-        z_tiles = {}
-        gate_tiles = {}
+        z_banks = {}
+        zs_tiles = {}
         ig_tiles = {}
+        fc_tiles = {}
         cn_tiles = {}
         th_tiles = {}
-        ht_tiles = {}
-        ot_tiles = {}
+        hn_tiles = {}
 
-        def load_x(c):
-            x_sb = xpool.tile([P, NT * I], BF16, name="x_sb")
-            nc.sync.dma_start(
-                out=x_sb[:].rearrange("p (n k) -> p n k", n=NT),
-                in_=x_rows[c * ROWS:(c + 1) * ROWS, :].rearrange("(n p) k -> p n k", p=P),
-            )
+        def load_x(c, parts):
+            x_sb = xpool.tile([P, TC * I], BF16, name="x_sb")
+            step = TC // parts
+            for k in range(parts):
+                nc.sync.dma_start(
+                    out=x_sb[:, k * step * I:(k + 1) * step * I],
+                    in_=inputs[:, c * TC + k * step:c * TC + (k + 1) * step, :].rearrange("b t k -> b (t k)"),
+                )
             x_tiles[c] = x_sb
 
         w_sb = consts.tile([P, 4 * I], BF16, name="w_sb")
         for q in range(4):
             nc.sync.dma_start(out=w_sb[:, q * I:(q + 1) * I], in_=w_in[q])
-        load_x(0)
-        small = consts.tile([P, 6 * H], BF16, name="small")
+        load_x(0, TC)
+        small = consts.tile([P, 5 * H], BF16, name="small")
         nc.sync.dma_start(out=small[:, 0:H], in_=h0[0])
         for q in range(4):
             nc.sync.dma_start(out=small[:, (q + 1) * H:(q + 2) * H], in_=w_hid[q])
-        nc.sync.dma_start(out=small[:, 5 * H:6 * H], in_=c0[0])
-        load_x(1)
+        load_x(1, 1)
         brow = consts.tile([P, G4], BF16, name="brow")
         nc.vector.memset(brow[:].bitcast(I32), 0)
         for q in range(4):
             nc.sync.dma_start(out=brow[0:1, q * H:(q + 1) * H], in_=b_in[q].rearrange("h o -> o h"))
             nc.sync.dma_start(out=brow[1:2, q * H:(q + 1) * H], in_=b_hid[q].rearrange("h o -> o h"))
+        c0_bf = consts.tile([P, H], BF16, name="c0_bf")
+        nc.sync.dma_start(out=c0_bf[:], in_=c0[0])
         for c in range(2, XBUFS):
-            load_x(c)
+            load_x(c, 1)
 
         ident_f = consts.tile([P, P], F32, name="ident_f")
         make_identity(nc, ident_f[:])
@@ -112,144 +109,158 @@ def tile_naivelstm_pa_t_kernel(
         w_words = w_sb[:].bitcast(F32)
         for q in range(4):
             bank = transpose_rows(w_words[:, q * 512:(q + 1) * 512])
-            copy_out(nc.vector.tensor_copy, wg_words[:, :, q * H:(q + 1) * H, :], bank)
+            copy_out(nc.vector.tensor_copy if q % 2 == 0 else nc.scalar.copy,
+                     wg_words[:, :, q * H:(q + 1) * H, :], bank)
         w_codes = consts.tile([P, 2 * G4], U32, name="w_codes", align_bytes=64)
         w_scales = consts.tile([P, 2 * G4], U8, name="w_scales", align_bytes=64)
         nc.vector.quantize_mx(out=w_codes[:].bitcast(FP8X4), scales=w_scales[:], in_=wg[:])
 
-        rt_sb = consts.tile([P, G4], F32, name="rt_sb")
-        c0t = consts.tile([P, B], F32, name="c0t")
-        clt = consts.tile([P, B], F32, name="clt")
+        r_sb = consts.tile([P, G4], F32, name="r_sb")
+        c0_f = consts.tile([P, H], F32, name="c0_f")
 
         def make_r():
-            small_ps = ps_t.tile([P, 6 * H], BF16, name="small_ps", tag="bank")
-            for s in range(6):
+            small_ps = ps_z.tile([P, 5 * H], BF16, name="small_ps", tag="z_ps")
+            for s in range(5):
                 nc.tensor.transpose(small_ps[:, s * H:(s + 1) * H], small[:, s * H:(s + 1) * H], ident_b[:])
-            small_t = consts.tile([P, 6 * H], BF16, name="small_t")
+            small_t = consts.tile([P, 5 * H], BF16, name="small_t")
             nc.vector.tensor_copy(out=small_t[:], in_=small_ps[:])
-            rt_ps = ps_o.tile([P, G4], F32, name="rt_ps", tag="ot")
-            for q in range(4):
-                cols = slice(q * H, (q + 1) * H)
-                nc.tensor.matmul(rt_ps[:, cols], lhsT=small_t[:, (q + 1) * H:(q + 2) * H], rhs=small_t[:, 0:H],
-                                 start=True, stop=False)
-                nc.tensor.matmul(rt_ps[:, cols], lhsT=brow[:, cols], rhs=ones[:], start=False, stop=True)
-            nc.vector.tensor_copy(out=rt_sb[:], in_=rt_ps[:])
-            nc.vector.tensor_copy(out=c0t[:], in_=small_t[:, 5 * H:6 * H])
+            r_ps = ps_z.tile([P, G4], F32, name="r_ps", tag="z_ps")
+            nc.tensor.matmul(r_ps[:], lhsT=small_t[:, 0:H], rhs=small_t[:, H:5 * H], start=True, stop=False)
+            nc.tensor.matmul(r_ps[:], lhsT=ones[:], rhs=brow[:], start=False, stop=True)
+            nc.vector.tensor_copy(out=r_sb[:], in_=r_ps[:])
+            nc.vector.tensor_copy(out=c0_f[:], in_=c0_bf[:])
 
         def stage_tp(c):
             x_words = x_tiles[c][:].bitcast(F32)
-            xg = gpool.tile([P, 2 * ROWS * 4], BF16, name="xg", align_bytes=64)
-            xg_words = xg[:].bitcast(F32).rearrange("p (g c u) -> p g c u", g=2, c=ROWS, u=2)
-            for n in range(NT):
-                bank = transpose_rows(x_words[:, n * 512:(n + 1) * 512])
-                copy_out(nc.scalar.copy if n < 2 else nc.vector.tensor_copy,
-                         xg_words[:, :, n * P:(n + 1) * P, :], bank)
-            xg_tiles[c] = xg
+            bank_tiles[c] = [transpose_rows(x_words[:, j * 512:(j + 1) * 512]) for j in range(TC)]
             if c + XBUFS < NCH:
-                load_x(c + XBUFS)
+                load_x(c + XBUFS, 1)
+
+        def stage_copy(c, share_with_vector):
+            xg = gpool.tile([P, TC * 2 * P * 4], BF16, name="xg", align_bytes=64)
+            xg_words = xg[:].bitcast(F32).rearrange("p (j g c u) -> p j g c u", j=TC, g=2, c=P, u=2)
+            for j in range(TC):
+                on_vector = share_with_vector and j % 2 == 1
+                copy_out(nc.vector.tensor_copy if on_vector else nc.scalar.copy, xg_words[:, j], bank_tiles[c][j])
+            xg_tiles[c] = xg
 
         def stage_q(c):
-            x_codes = qpool.tile([P, 2 * ROWS], U32, name="x_codes", align_bytes=64)
-            x_scales = qpool.tile([P, 2 * ROWS], U8, name="x_scales", align_bytes=64)
+            x_codes = qpool.tile([P, TC * 2 * P], U32, name="x_codes", align_bytes=64)
+            x_scales = qpool.tile([P, TC * 2 * P], U8, name="x_scales", align_bytes=64)
             nc.vector.quantize_mx(out=x_codes[:].bitcast(FP8X4), scales=x_scales[:], in_=xg_tiles[c][:])
             code_tiles[c] = (x_codes, x_scales)
 
         def stage_mx(c):
             x_codes, x_scales = code_tiles[c]
             banks = []
-            for q in range(4):
-                z_ps = ps_z.tile([P, ROWS], F32, name="z_ps%d" % q, tag="z_ps%d" % q)
+            for j in range(TC):
+                z_ps = ps_z.tile([P, G4], F32, name="z_ps", tag="z_ps")
                 for g in range(2):
-                    w_cols = slice(g * G4 + q * H, g * G4 + (q + 1) * H)
-                    x_cols = slice(g * ROWS, (g + 1) * ROWS)
+                    cols = slice((j * 2 + g) * P, (j * 2 + g + 1) * P)
                     nc.tensor.matmul_mx(
                         out=z_ps[:],
-                        lhsT=w_codes[:, w_cols].bitcast(FP8X4),
-                        lhsT_scale=w_scales[:, w_cols],
-                        rhs=x_codes[:, x_cols].bitcast(FP8X4),
-                        rhs_scale=x_scales[:, x_cols],
+                        lhsT=x_codes[:, cols].bitcast(FP8X4),
+                        lhsT_scale=x_scales[:, cols],
+                        rhs=w_codes[:, g * G4:(g + 1) * G4].bitcast(FP8X4),
+                        rhs_scale=w_scales[:, g * G4:(g + 1) * G4],
                         start=(g == 0),
                         stop=(g == 1),
                     )
                 banks.append(z_ps)
-            z_tiles[c] = banks
+            z_banks[c] = banks
 
-        def stage_act(c):
-            gates = []
-            for q in range(4):
-                gate = spool.tile([P, ROWS], F32, name="gate%d" % q, tag="gate%d" % q)
-                for bl in range(NB):
-                    cols = slice(bl * T, (bl + 1) * T)
-                    b = c * NB + bl
-                    nc.scalar.activation(out=gate[:, cols], in_=z_tiles[c][q][:, cols], func=funcs[q],
-                                         bias=rt_sb[:, q * B + b:q * B + b + 1])
-                gates.append(gate)
-            gate_tiles[c] = gates
+        def stage_add_r(c):
+            zs = zpool.tile([P, TC, G4], F32, name="zs")
+            for j in range(TC):
+                nc.vector.tensor_tensor(out=zs[:, j, :], in0=z_banks[c][j][:], in1=r_sb[:], op=ALU.add)
+            zs_tiles[c] = zs
 
-        def stage_cell(c):
-            g_i, g_g, g_f, g_o = gate_tiles[c]
-            ig = epool.tile([P, ROWS], F32, name="ig")
-            nc.vector.tensor_tensor(out=ig[:], in0=g_i[:], in1=g_g[:], op=ALU.mult)
-            cn = epool.tile([P, ROWS], F32, name="cn")
-            for bl in range(NB):
-                cols = slice(bl * T, (bl + 1) * T)
-                b = c * NB + bl
-                nc.vector.scalar_tensor_tensor(out=cn[:, cols], in0=g_f[:, cols], scalar=c0t[:, b:b + 1],
-                                               in1=ig[:, cols], op0=ALU.mult, op1=ALU.add)
-            nc.vector.tensor_copy(out=clt[:, c * NB:(c + 1) * NB],
-                                  in_=cn[:].rearrange("p (b t) -> p b t", t=T)[:, :, T - 1])
-            cn_tiles[c] = cn
+        def stage_act(c, span):
+            js = slice(span[0], span[1])
+            zs = zs_tiles[c]
+            nc.scalar.activation(out=zs[:, js, 0:3 * H], in_=zs[:, js, 0:3 * H], func=ACT.Sigmoid)
+            nc.scalar.activation(out=zs[:, js, 3 * H:G4], in_=zs[:, js, 3 * H:G4], func=ACT.Tanh)
 
-        def stage_tanh_c(c):
-            th = epool.tile([P, ROWS], F32, name="th")
-            nc.scalar.activation(out=th[:], in_=cn_tiles[c][:], func=ACT.Tanh)
-            th_tiles[c] = th
+        def stage_products(c, span, engine):
+            js = slice(span[0], span[1])
+            zs = zs_tiles[c]
+            if c not in ig_tiles:
+                ig_tiles[c] = ppool.tile([P, TC, H], F32, name="ig")
+                fc_tiles[c] = ppool.tile([P, TC, H], F32, name="fc")
+            n = span[1] - span[0]
+            engine.tensor_tensor(out=ig_tiles[c][:, js, :], in0=zs[:, js, 0:H], in1=zs[:, js, 3 * H:G4], op=ALU.mult)
+            engine.tensor_tensor(out=fc_tiles[c][:, js, :], in0=zs[:, js, H:2 * H],
+                                 in1=c0_f[:].unsqueeze(1).to_broadcast([P, n, H]), op=ALU.mult)
 
-        def stage_h(c):
-            ht = epool.tile([P, ROWS], F32, name="ht")
-            nc.vector.tensor_tensor(out=ht[:], in0=gate_tiles[c][3][:], in1=th_tiles[c][:], op=ALU.mult)
-            ht_tiles[c] = ht
+        def stage_sum(c, span):
+            js = slice(span[0], span[1])
+            if c not in cn_tiles:
+                cn_tiles[c] = epool.tile([P, TC, H], F32, name="cn")
+            nc.vector.tensor_tensor(out=cn_tiles[c][:, js, :], in0=fc_tiles[c][:, js, :], in1=ig_tiles[c][:, js, :],
+                                    op=ALU.add)
 
-        def stage_ot(c):
-            ot = ps_o.tile([P, ROWS], F32, name="ot", tag="ot")
-            for n in range(NT):
-                nc.tensor.transpose(ot[:, n * P:(n + 1) * P], ht_tiles[c][:, n * P:(n + 1) * P], ident_f[:])
-            ot_tiles[c] = ot
+        def stage_tanh_c(c, span):
+            js = slice(span[0], span[1])
+            if c not in th_tiles:
+                th_tiles[c] = epool.tile([P, TC, H], F32, name="th")
+            nc.scalar.activation(out=th_tiles[c][:, js, :], in_=cn_tiles[c][:, js, :], func=ACT.Tanh)
 
-        def stage_store(c):
-            o_sb = epool.tile([P, NT, H], F32, name="o_sb")
-            nc.vector.tensor_copy(out=o_sb[:].rearrange("p n h -> p (n h)"), in_=ot_tiles[c][:])
-            for e in range(2):
-                nc.sync.dma_start(out=out_seq[e, :, c * NT:(c + 1) * NT, :], in_=o_sb[e * T:(e + 1) * T, :, :])
-            nc.sync.dma_start(out=out_hl[:, c * NT:(c + 1) * NT, :], in_=o_sb[T - 1:P:T, :, :])
+        def stage_out(c, span):
+            js = slice(span[0], span[1])
+            if c not in hn_tiles:
+                hn_tiles[c] = epool.tile([P, TC, H], F32, name="hn")
+            hn = hn_tiles[c]
+            nc.vector.tensor_tensor(out=hn[:, js, :], in0=zs_tiles[c][:, js, 2 * H:3 * H], in1=th_tiles[c][:, js, :],
+                                    op=ALU.mult)
+            nc.sync.dma_start(out=out_0[c * TC + span[0]:c * TC + span[1]].rearrange("t b h -> b t h"),
+                              in_=hn[:, js, :])
 
         def live(c):
             return 0 <= c < NCH
 
-        for i in range(-1, NCH + 4):
+        whole = (0, TC)
+
+        stage_tp(0)
+        stage_copy(0, True)
+        stage_q(0)
+        stage_tp(1)
+        stage_copy(1, True)
+        make_r()
+
+        for i in range(NCH):
+            stage_mx(i)
+            if live(i + 2):
+                stage_tp(i + 2)
             if live(i - 1):
-                stage_cell(i - 1)
-            if live(i + 1):
-                stage_tp(i + 1)
-            if i == -1:
-                make_r()
-            if live(i - 3):
-                stage_ot(i - 3)
-            if live(i):
-                stage_mx(i)
-            if live(i - 2):
-                stage_h(i - 2)
+                stage_act(i - 1, whole)
             if live(i + 1):
                 stage_q(i + 1)
             if live(i - 3):
-                stage_store(i - 3)
-            if live(i):
-                stage_act(i)
+                stage_out(i - 3, whole)
+            if live(i - 2):
+                stage_sum(i - 2, whole)
             if live(i - 1):
-                stage_tanh_c(i - 1)
-            if i == NCH:
-                cl_ps = ps_t.tile([P, H], F32, name="cl_ps", tag="bank")
-                nc.tensor.transpose(cl_ps[:], clt[:], ident_f[:])
-                cl_sb = consts.tile([P, H], F32, name="cl_sb")
-                nc.scalar.copy(out=cl_sb[:], in_=cl_ps[:])
-                nc.sync.dma_start(out=out_2[0], in_=cl_sb[:])
+                stage_products(i - 1, whole, nc.gpsimd)
+            stage_add_r(i)
+            if live(i + 2):
+                stage_copy(i + 2, False)
+            if live(i - 2):
+                stage_tanh_c(i - 2, whole)
+
+        last = NCH - 1
+        halves = [(0, TC // 2), (TC // 2, TC)]
+        for js in halves:
+            stage_act(last, js)
+        stage_sum(last - 1, whole)
+        stage_tanh_c(last - 1, whole)
+        stage_out(last - 2, whole)
+        for js in halves:
+            stage_products(last, js, nc.vector)
+            stage_sum(last, js)
+            stage_tanh_c(last, js)
+            if js[0] == 0:
+                stage_out(last - 1, whole)
+        nc.sync.dma_start(out=out_2[0], in_=cn_tiles[last][:, TC - 1, :])
+        for js in halves:
+            stage_out(last, js)
+        nc.sync.dma_start(out=out_1[0], in_=hn_tiles[last][:, TC - 1, :])

@@ -40,7 +40,7 @@ def tile_naivelstm_pa_t_kernel(
         ppool = ctx.enter_context(tc.tile_pool(name="ppool", bufs=1))
         epool = ctx.enter_context(tc.tile_pool(name="epool", bufs=3))
         ps_t = ctx.enter_context(tc.psum_pool(name="ps_t", bufs=4))
-        ps_z = ctx.enter_context(tc.psum_pool(name="ps_z", bufs=4))
+        ps_z = ctx.enter_context(tc.psum_pool(name="ps_z", bufs=1))
         ctx.enter_context(tc.manual_schedule())
 
         x_tiles = {}
@@ -109,8 +109,7 @@ def tile_naivelstm_pa_t_kernel(
         w_words = w_sb[:].bitcast(F32)
         for q in range(4):
             bank = transpose_rows(w_words[:, q * 512:(q + 1) * 512])
-            copy_out(nc.vector.tensor_copy if q % 2 == 0 else nc.scalar.copy,
-                     wg_words[:, :, q * H:(q + 1) * H, :], bank)
+            copy_out(nc.scalar.copy, wg_words[:, :, q * H:(q + 1) * H, :], bank)
         w_codes = consts.tile([P, 2 * G4], U32, name="w_codes", align_bytes=64)
         w_scales = consts.tile([P, 2 * G4], U8, name="w_scales", align_bytes=64)
         nc.vector.quantize_mx(out=w_codes[:].bitcast(FP8X4), scales=w_scales[:], in_=wg[:])
@@ -119,16 +118,16 @@ def tile_naivelstm_pa_t_kernel(
         c0_f = consts.tile([P, H], F32, name="c0_f")
 
         def make_r():
-            small_ps = ps_z.tile([P, 5 * H], BF16, name="small_ps", tag="z_ps")
+            small_ps = ps_z.tile([P, 5 * H], BF16, name="small_ps", tag="z_ps0")
             for s in range(5):
                 nc.tensor.transpose(small_ps[:, s * H:(s + 1) * H], small[:, s * H:(s + 1) * H], ident_b[:])
             small_t = consts.tile([P, 5 * H], BF16, name="small_t")
-            nc.vector.tensor_copy(out=small_t[:], in_=small_ps[:])
-            r_ps = ps_z.tile([P, G4], F32, name="r_ps", tag="z_ps")
+            nc.scalar.copy(out=small_t[:], in_=small_ps[:])
+            r_ps = ps_z.tile([P, G4], F32, name="r_ps", tag="z_ps1")
             nc.tensor.matmul(r_ps[:], lhsT=small_t[:, 0:H], rhs=small_t[:, H:5 * H], start=True, stop=False)
             nc.tensor.matmul(r_ps[:], lhsT=ones[:], rhs=brow[:], start=False, stop=True)
-            nc.vector.tensor_copy(out=r_sb[:], in_=r_ps[:])
-            nc.vector.tensor_copy(out=c0_f[:], in_=c0_bf[:])
+            nc.scalar.copy(out=r_sb[:], in_=r_ps[:])
+            nc.scalar.copy(out=c0_f[:], in_=c0_bf[:])
 
         def stage_tp(c):
             x_words = x_tiles[c][:].bitcast(F32)
@@ -136,12 +135,11 @@ def tile_naivelstm_pa_t_kernel(
             if c + XBUFS < NCH:
                 load_x(c + XBUFS, 1)
 
-        def stage_copy(c, share_with_vector):
+        def stage_copy(c):
             xg = gpool.tile([P, TC * 2 * P * 4], BF16, name="xg", align_bytes=64)
             xg_words = xg[:].bitcast(F32).rearrange("p (j g c u) -> p j g c u", j=TC, g=2, c=P, u=2)
             for j in range(TC):
-                on_vector = share_with_vector and j % 2 == 1
-                copy_out(nc.vector.tensor_copy if on_vector else nc.scalar.copy, xg_words[:, j], bank_tiles[c][j])
+                copy_out(nc.scalar.copy, xg_words[:, j], bank_tiles[c][j])
             xg_tiles[c] = xg
 
         def stage_q(c):
@@ -150,11 +148,14 @@ def tile_naivelstm_pa_t_kernel(
             nc.vector.quantize_mx(out=x_codes[:].bitcast(FP8X4), scales=x_scales[:], in_=xg_tiles[c][:])
             code_tiles[c] = (x_codes, x_scales)
 
+        def fill_order(c):
+            return list(range(TC)) if c % 2 == 0 else list(reversed(range(TC)))
+
         def stage_mx(c):
             x_codes, x_scales = code_tiles[c]
-            banks = []
-            for j in range(TC):
-                z_ps = ps_z.tile([P, G4], F32, name="z_ps", tag="z_ps")
+            banks = {}
+            for j in fill_order(c):
+                z_ps = ps_z.tile([P, G4], F32, name="z_ps%d" % j, tag="z_ps%d" % j)
                 for g in range(2):
                     cols = slice((j * 2 + g) * P, (j * 2 + g + 1) * P)
                     nc.tensor.matmul_mx(
@@ -166,12 +167,12 @@ def tile_naivelstm_pa_t_kernel(
                         start=(g == 0),
                         stop=(g == 1),
                     )
-                banks.append(z_ps)
+                banks[j] = z_ps
             z_banks[c] = banks
 
         def stage_add_r(c):
             zs = zpool.tile([P, TC, G4], F32, name="zs")
-            for j in range(TC):
+            for j in reversed(fill_order(c)):
                 nc.vector.tensor_tensor(out=zs[:, j, :], in0=z_banks[c][j][:], in1=r_sb[:], op=ALU.add)
             zs_tiles[c] = zs
 
@@ -192,12 +193,12 @@ def tile_naivelstm_pa_t_kernel(
             engine.tensor_tensor(out=fc_tiles[c][:, js, :], in0=zs[:, js, H:2 * H],
                                  in1=c0_f[:].unsqueeze(1).to_broadcast([P, n, H]), op=ALU.mult)
 
-        def stage_sum(c, span):
+        def stage_sum(c, span, engine):
             js = slice(span[0], span[1])
             if c not in cn_tiles:
                 cn_tiles[c] = epool.tile([P, TC, H], F32, name="cn")
-            nc.vector.tensor_tensor(out=cn_tiles[c][:, js, :], in0=fc_tiles[c][:, js, :], in1=ig_tiles[c][:, js, :],
-                                    op=ALU.add)
+            engine.tensor_tensor(out=cn_tiles[c][:, js, :], in0=fc_tiles[c][:, js, :], in1=ig_tiles[c][:, js, :],
+                                 op=ALU.add)
 
         def stage_tanh_c(c, span):
             js = slice(span[0], span[1])
@@ -221,10 +222,10 @@ def tile_naivelstm_pa_t_kernel(
         whole = (0, TC)
 
         stage_tp(0)
-        stage_copy(0, True)
+        stage_copy(0)
         stage_q(0)
         stage_tp(1)
-        stage_copy(1, True)
+        stage_copy(1)
         make_r()
 
         for i in range(NCH):
@@ -233,17 +234,16 @@ def tile_naivelstm_pa_t_kernel(
                 stage_tp(i + 2)
             if live(i - 1):
                 stage_act(i - 1, whole)
-            if live(i + 1):
-                stage_q(i + 1)
             if live(i - 3):
                 stage_out(i - 3, whole)
-            if live(i - 2):
-                stage_sum(i - 2, whole)
+            if live(i + 1):
+                stage_q(i + 1)
             if live(i - 1):
                 stage_products(i - 1, whole, nc.gpsimd)
+                stage_sum(i - 1, whole, nc.gpsimd)
             stage_add_r(i)
             if live(i + 2):
-                stage_copy(i + 2, False)
+                stage_copy(i + 2)
             if live(i - 2):
                 stage_tanh_c(i - 2, whole)
 
@@ -251,12 +251,11 @@ def tile_naivelstm_pa_t_kernel(
         halves = [(0, TC // 2), (TC // 2, TC)]
         for js in halves:
             stage_act(last, js)
-        stage_sum(last - 1, whole)
         stage_tanh_c(last - 1, whole)
         stage_out(last - 2, whole)
         for js in halves:
             stage_products(last, js, nc.vector)
-            stage_sum(last, js)
+            stage_sum(last, js, nc.vector)
             stage_tanh_c(last, js)
             if js[0] == 0:
                 stage_out(last - 1, whole)

@@ -186,19 +186,20 @@ def tile_naivelstm_pa_t_kernel(
             js = slice(span[0], span[1])
             zs = zs_tiles[c]
             if c not in ig_tiles:
-                ig_tiles[c] = ppool.tile([P, TC, H], F32, name="ig")
-                fc_tiles[c] = ppool.tile([P, TC, H], F32, name="fc")
+                kind = "_last" if c == NCH - 1 else ""
+                ig_tiles[c] = ppool.tile([P, TC, H], F32, name="ig" + kind)
+                fc_tiles[c] = ppool.tile([P, TC, H], F32, name="fc" + kind)
             n = span[1] - span[0]
             engine.tensor_tensor(out=ig_tiles[c][:, js, :], in0=zs[:, js, 0:H], in1=zs[:, js, 3 * H:G4], op=ALU.mult)
             engine.tensor_tensor(out=fc_tiles[c][:, js, :], in0=zs[:, js, H:2 * H],
                                  in1=c0_f[:].unsqueeze(1).to_broadcast([P, n, H]), op=ALU.mult)
 
-        def stage_sum(c, span, engine):
+        def stage_sum(c, span):
             js = slice(span[0], span[1])
             if c not in cn_tiles:
                 cn_tiles[c] = epool.tile([P, TC, H], F32, name="cn")
-            engine.tensor_tensor(out=cn_tiles[c][:, js, :], in0=fc_tiles[c][:, js, :], in1=ig_tiles[c][:, js, :],
-                                 op=ALU.add)
+            nc.vector.tensor_tensor(out=cn_tiles[c][:, js, :], in0=fc_tiles[c][:, js, :], in1=ig_tiles[c][:, js, :],
+                                    op=ALU.add)
 
         def stage_tanh_c(c, span):
             js = slice(span[0], span[1])
@@ -238,9 +239,10 @@ def tile_naivelstm_pa_t_kernel(
                 stage_out(i - 3, whole)
             if live(i + 1):
                 stage_q(i + 1)
+            if live(i - 2):
+                stage_sum(i - 2, whole)
             if live(i - 1):
                 stage_products(i - 1, whole, nc.gpsimd)
-                stage_sum(i - 1, whole, nc.gpsimd)
             stage_add_r(i)
             if live(i + 2):
                 stage_copy(i + 2)
@@ -251,11 +253,12 @@ def tile_naivelstm_pa_t_kernel(
         halves = [(0, TC // 2), (TC // 2, TC)]
         for js in halves:
             stage_act(last, js)
-        stage_tanh_c(last - 1, whole)
         stage_out(last - 2, whole)
+        stage_sum(last - 1, whole)
+        stage_tanh_c(last - 1, whole)
         for js in halves:
             stage_products(last, js, nc.vector)
-            stage_sum(last, js, nc.vector)
+            stage_sum(last, js)
             stage_tanh_c(last, js)
             if js[0] == 0:
                 stage_out(last - 1, whole)

@@ -139,7 +139,8 @@ def tile_naivelstm_pa_t_kernel(
             xg = gpool.tile([P, TC * 2 * P * 4], BF16, name="xg", align_bytes=64)
             xg_words = xg[:].bitcast(F32).rearrange("p (j g c u) -> p j g c u", j=TC, g=2, c=P, u=2)
             for j in range(TC):
-                copy_out(nc.scalar.copy, xg_words[:, j], bank_tiles[c][j])
+                on_vector = c >= 2 and c % 2 == 1 and j == TC - 1
+                copy_out(nc.vector.tensor_copy if on_vector else nc.scalar.copy, xg_words[:, j], bank_tiles[c][j])
             xg_tiles[c] = xg
 
         def stage_q(c):

from contextlib import ExitStack

import concourse.mybir as mybir
from concourse.masks import make_identity

FP8X4 = mybir.dt.float8_e4m3fn_x4
BF16 = mybir.dt.bfloat16
F32 = mybir.dt.float32
I32 = mybir.dt.int32
U32 = mybir.dt.uint32
U8 = mybir.dt.uint8
ACT = mybir.ActivationFunctionType
ALU = mybir.AluOpType

B, T, I, H = 128, 64, 1024, 128
P = 128
G4 = 4 * H
TC = 4
NCH = T // TC
XBUFS = 8
FLOPS = 2 * B * T * I * G4 + 2 * B * H * G4


def tile_naivelstm_pa_t_kernel(
    tc, inputs, h0, c0, w_ii, b_ii, w_hi, b_hi, w_if_, b_if_, w_hf, b_hf,
    w_io, b_io, w_ho, b_ho, w_ig, b_ig, w_hg, b_hg, out_0, out_1, out_2,
):
    nc = tc.nc
    w_in = [w_ii, w_if_, w_io, w_ig]
    w_hid = [w_hi, w_hf, w_ho, w_hg]
    b_in = [b_ii, b_if_, b_io, b_ig]
    b_hid = [b_hi, b_hf, b_ho, b_hg]

    with ExitStack() as ctx:
        consts = ctx.enter_context(tc.tile_pool(name="consts", bufs=1))
        xpool = ctx.enter_context(tc.tile_pool(name="xpool", bufs=XBUFS))
        gpool = ctx.enter_context(tc.tile_pool(name="gpool", bufs=3))
        qpool = ctx.enter_context(tc.tile_pool(name="qpool", bufs=3))
        zpool = ctx.enter_context(tc.tile_pool(name="zpool", bufs=4))
        ppool = ctx.enter_context(tc.tile_pool(name="ppool", bufs=1))
        epool = ctx.enter_context(tc.tile_pool(name="epool", bufs=3))
        ps_t = ctx.enter_context(tc.psum_pool(name="ps_t", bufs=4))
        ps_z = ctx.enter_context(tc.psum_pool(name="ps_z", bufs=1))
        ctx.enter_context(tc.manual_schedule())

        x_tiles = {}
        bank_tiles = {}
        xg_tiles = {}
        code_tiles = {}
        z_banks = {}
        zs_tiles = {}
        ig_tiles = {}
        fc_tiles = {}
        cn_tiles = {}
        th_tiles = {}
        hn_tiles = {}

        def load_x(c, parts):
            x_sb = xpool.tile([P, TC * I], BF16, name="x_sb")
            step = TC // parts
            for k in range(parts):
                nc.sync.dma_start(
                    out=x_sb[:, k * step * I:(k + 1) * step * I],
                    in_=inputs[:, c * TC + k * step:c * TC + (k + 1) * step, :].rearrange("b t k -> b (t k)"),
                )
            x_tiles[c] = x_sb

        w_sb = consts.tile([P, 4 * I], BF16, name="w_sb")
        for q in range(4):
            nc.sync.dma_start(out=w_sb[:, q * I:(q + 1) * I], in_=w_in[q])
        load_x(0, TC)
        small = consts.tile([P, 5 * H], BF16, name="small")
        nc.sync.dma_start(out=small[:, 0:H], in_=h0[0])
        for q in range(4):
            nc.sync.dma_start(out=small[:, (q + 1) * H:(q + 2) * H], in_=w_hid[q])
        load_x(1, 1)
        brow = consts.tile([P, G4], BF16, name="brow")
        nc.vector.memset(brow[:].bitcast(I32), 0)
        for q in range(4):
            nc.sync.dma_start(out=brow[0:1, q * H:(q + 1) * H], in_=b_in[q].rearrange("h o -> o h"))
            nc.sync.dma_start(out=brow[1:2, q * H:(q + 1) * H], in_=b_hid[q].rearrange("h o -> o h"))
        c0_bf = consts.tile([P, H], BF16, name="c0_bf")
        nc.sync.dma_start(out=c0_bf[:], in_=c0[0])
        for c in range(2, XBUFS):
            load_x(c, 1)

        ident_f = consts.tile([P, P], F32, name="ident_f")
        make_identity(nc, ident_f[:])
        ident_b = consts.tile([P, P], BF16, name="ident_b")
        make_identity(nc, ident_b[:])
        ones = consts.tile([P, P], BF16, name="ones")
        nc.vector.memset(ones[:], 1.0)
        warm = consts.tile([P, 1], F32, name="warm")
        nc.vector.memset(warm[:], 0.0)
        warm_out = consts.tile([P, 1], F32, name="warm_out")
        nc.scalar.activation(out=warm_out[:], in_=warm[:], func=ACT.Sigmoid)

        def transpose_rows(words):
            bank = ps_t.tile([P, 4 * P], F32, name="bank", tag="bank")
            for s in range(4):
                nc.tensor.transpose(bank[:, s * P:(s + 1) * P], words[:, s * P:(s + 1) * P], ident_f[:])
            return bank

        def copy_out(engine_copy, dst_words, bank):
            engine_copy(out=dst_words, in_=bank[:].rearrange("p (g u c) -> p g c u", g=2, u=2, c=P))

        wg = consts.tile([P, 2 * G4 * 4], BF16, name="wg", align_bytes=64)
        wg_words = wg[:].bitcast(F32).rearrange("p (g c u) -> p g c u", g=2, c=G4, u=2)
        w_words = w_sb[:].bitcast(F32)
        for q in range(4):
            bank = transpose_rows(w_words[:, q * 512:(q + 1) * 512])
            copy_out(nc.scalar.copy, wg_words[:, :, q * H:(q + 1) * H, :], bank)
        w_codes = consts.tile([P, 2 * G4], U32, name="w_codes", align_bytes=64)
        w_scales = consts.tile([P, 2 * G4], U8, name="w_scales", align_bytes=64)
        nc.vector.quantize_mx(out=w_codes[:].bitcast(FP8X4), scales=w_scales[:], in_=wg[:])

        r_sb = consts.tile([P, G4], F32, name="r_sb")
        c0_f = consts.tile([P, H], F32, name="c0_f")

        def make_r():
            small_ps = ps_z.tile([P, 5 * H], BF16, name="small_ps", tag="z_ps0")
            for s in range(5):
                nc.tensor.transpose(small_ps[:, s * H:(s + 1) * H], small[:, s * H:(s + 1) * H], ident_b[:])
            small_t = consts.tile([P, 5 * H], BF16, name="small_t")
            nc.scalar.copy(out=small_t[:], in_=small_ps[:])
            r_ps = ps_z.tile([P, G4], F32, name="r_ps", tag="z_ps1")
            nc.tensor.matmul(r_ps[:], lhsT=small_t[:, 0:H], rhs=small_t[:, H:5 * H], start=True, stop=False)
            nc.tensor.matmul(r_ps[:], lhsT=ones[:], rhs=brow[:], start=False, stop=True)
            nc.scalar.copy(out=r_sb[:], in_=r_ps[:])
            nc.scalar.copy(out=c0_f[:], in_=c0_bf[:])

        def stage_tp(c):
            x_words = x_tiles[c][:].bitcast(F32)
            bank_tiles[c] = [transpose_rows(x_words[:, j * 512:(j + 1) * 512]) for j in range(TC)]
            if c + XBUFS < NCH:
                load_x(c + XBUFS, 1)

        def stage_copy(c):
            xg = gpool.tile([P, TC * 2 * P * 4], BF16, name="xg", align_bytes=64)
            xg_words = xg[:].bitcast(F32).rearrange("p (j g c u) -> p j g c u", j=TC, g=2, c=P, u=2)
            for j in range(TC):
                on_vector = c >= 2 and c % 2 == 1 and j == TC - 1
                copy_out(nc.vector.tensor_copy if on_vector else nc.scalar.copy, xg_words[:, j], bank_tiles[c][j])
            xg_tiles[c] = xg

        def stage_q(c):
            x_codes = qpool.tile([P, TC * 2 * P], U32, name="x_codes", align_bytes=64)
            x_scales = qpool.tile([P, TC * 2 * P], U8, name="x_scales", align_bytes=64)
            nc.vector.quantize_mx(out=x_codes[:].bitcast(FP8X4), scales=x_scales[:], in_=xg_tiles[c][:])
            code_tiles[c] = (x_codes, x_scales)

        def fill_order(c):
            return list(range(TC)) if c % 2 == 0 else list(reversed(range(TC)))

        def stage_mx(c):
            x_codes, x_scales = code_tiles[c]
            banks = {}
            for j in fill_order(c):
                z_ps = ps_z.tile([P, G4], F32, name="z_ps%d" % j, tag="z_ps%d" % j)
                for g in range(2):
                    cols = slice((j * 2 + g) * P, (j * 2 + g + 1) * P)
                    nc.tensor.matmul_mx(
                        out=z_ps[:],
                        lhsT=x_codes[:, cols].bitcast(FP8X4),
                        lhsT_scale=x_scales[:, cols],
                        rhs=w_codes[:, g * G4:(g + 1) * G4].bitcast(FP8X4),
                        rhs_scale=w_scales[:, g * G4:(g + 1) * G4],
                        start=(g == 0),
                        stop=(g == 1),
                    )
                banks[j] = z_ps
            z_banks[c] = banks

        def stage_add_r(c):
            zs = zpool.tile([P, TC, G4], F32, name="zs")
            for j in reversed(fill_order(c)):
                nc.vector.tensor_tensor(out=zs[:, j, :], in0=z_banks[c][j][:], in1=r_sb[:], op=ALU.add)
            zs_tiles[c] = zs

        def stage_act(c, span):
            js = slice(span[0], span[1])
            zs = zs_tiles[c]
            nc.scalar.activation(out=zs[:, js, 0:3 * H], in_=zs[:, js, 0:3 * H], func=ACT.Sigmoid)
            nc.scalar.activation(out=zs[:, js, 3 * H:G4], in_=zs[:, js, 3 * H:G4], func=ACT.Tanh)

        def stage_products(c, span, engine):
            js = slice(span[0], span[1])
            zs = zs_tiles[c]
            if c not in ig_tiles:
                kind = "_last" if c == NCH - 1 else ""
                ig_tiles[c] = ppool.tile([P, TC, H], F32, name="ig" + kind)
                fc_tiles[c] = ppool.tile([P, TC, H], F32, name="fc" + kind)
            n = span[1] - span[0]
            engine.tensor_tensor(out=ig_tiles[c][:, js, :], in0=zs[:, js, 0:H], in1=zs[:, js, 3 * H:G4], op=ALU.mult)
            engine.tensor_tensor(out=fc_tiles[c][:, js, :], in0=zs[:, js, H:2 * H],
                                 in1=c0_f[:].unsqueeze(1).to_broadcast([P, n, H]), op=ALU.mult)

        def stage_sum(c, span):
            js = slice(span[0], span[1])
            if c not in cn_tiles:
                cn_tiles[c] = epool.tile([P, TC, H], F32, name="cn")
            nc.vector.tensor_tensor(out=cn_tiles[c][:, js, :], in0=fc_tiles[c][:, js, :], in1=ig_tiles[c][:, js, :],
                                    op=ALU.add)

        def stage_tanh_c(c, span):
            js = slice(span[0], span[1])
            if c not in th_tiles:
                th_tiles[c] = epool.tile([P, TC, H], F32, name="th")
            nc.scalar.activation(out=th_tiles[c][:, js, :], in_=cn_tiles[c][:, js, :], func=ACT.Tanh)

        def stage_out(c, span):
            js = slice(span[0], span[1])
            if c not in hn_tiles:
                hn_tiles[c] = epool.tile([P, TC, H], F32, name="hn")
            hn = hn_tiles[c]
            nc.vector.tensor_tensor(out=hn[:, js, :], in0=zs_tiles[c][:, js, 2 * H:3 * H], in1=th_tiles[c][:, js, :],
                                    op=ALU.mult)
            nc.sync.dma_start(out=out_0[c * TC + span[0]:c * TC + span[1]].rearrange("t b h -> b t h"),
                              in_=hn[:, js, :])

        def live(c):
            return 0 <= c < NCH

        whole = (0, TC)

        stage_tp(0)
        stage_copy(0)
        stage_q(0)
        stage_tp(1)
        stage_copy(1)
        make_r()

        for i in range(NCH):
            stage_mx(i)
            if live(i + 2):
                stage_tp(i + 2)
            if live(i - 1):
                stage_act(i - 1, whole)
            if live(i - 3):
                stage_out(i - 3, whole)
            if live(i + 1):
                stage_q(i + 1)
            if live(i - 2):
                stage_sum(i - 2, whole)
            if live(i - 1):
                stage_products(i - 1, whole, nc.gpsimd)
            stage_add_r(i)
            if live(i + 2):
                stage_copy(i + 2)
            if live(i - 2):
                stage_tanh_c(i - 2, whole)

        last = NCH - 1
        halves = [(0, TC // 2), (TC // 2, TC)]
        for js in halves:
            stage_act(last, js)
        stage_out(last - 2, whole)
        stage_sum(last - 1, whole)
        stage_tanh_c(last - 1, whole)
        for js in halves:
            stage_products(last, js, nc.vector)
            stage_sum(last, js)
            stage_tanh_c(last, js)
            if js[0] == 0:
                stage_out(last - 1, whole)
        nc.sync.dma_start(out=out_2[0], in_=cn_tiles[last][:, TC - 1, :])
        for js in halves:
            stage_out(last, js)
        nc.sync.dma_start(out=out_1[0], in_=hn_tiles[last][:, TC - 1, :])
